import numpy as np
import ml_dtypes


def mxq(x, axis, fmt="e4m3"):
    dtype, down = {"e4m3": (ml_dtypes.float8_e4m3fn, 7), "e5m2": (ml_dtypes.float8_e5m2, 14)}[fmt]
    v = np.moveaxis(np.asarray(x, np.float32).astype(ml_dtypes.bfloat16).astype(np.float64), axis, -1)
    blocks = v.reshape(v.shape[:-1] + (-1, 32))
    amax = np.abs(blocks).max(-1, keepdims=True)
    byte = np.maximum(np.where(amax > 0, np.frexp(amax)[1] - 1 + 127, 0) - down, 1)
    scale = np.exp2(byte - 127.0)
    codes = (blocks / scale).astype(np.float32).astype(dtype).astype(np.float64)
    return np.moveaxis((codes * scale).reshape(v.shape), -1, axis)


WIDE = False


def mx_kscale(k):
    if not WIDE:
        return np.ones(k)
    levels = np.array([10, -10, 5, -5, 0])
    if k % 512:
        return np.exp2(np.random.permutation(np.resize(levels, k // 32))).repeat(32)
    a = np.empty((k // 512, 16))
    for p in range(k // 512):
        a[p, :8] = np.random.permutation(np.resize(levels, 8))
        for g in range(8):
            far = levels[np.abs(levels - a[p, g]) >= 10]
            a[p, g + 8] = far[np.random.randint(len(far))]
    return np.exp2(a.ravel()).repeat(32)


BF16 = ml_dtypes.bfloat16


def bf(x):
    return np.asarray(x, np.float32).astype(BF16)


def f64(x):
    return np.asarray(x).astype(np.float64)


B, C, M, O, H, W = 4, 512, 512, 512, 32, 32
H2, W2 = H // 2, W // 2
KS = 3
PAD = KS // 2
BN_EPS = 1e-5


def haar_ll(x):
    a = x[:, :, 0::2, 0::2]
    b = x[:, :, 0::2, 1::2]
    c = x[:, :, 1::2, 0::2]
    d = x[:, :, 1::2, 1::2]
    return (a + b + c + d) * 0.5


def windows(u):
    up = np.pad(u, ((0, 0), (0, 0), (PAD, PAD), (PAD, PAD)))
    return np.stack([up[:, :, i:i + H2, j:j + W2] for i in range(KS) for j in range(KS)], axis=-1)


def setup_inputs():
    s, t = mx_kscale(C), mx_kscale(M)
    return {
        "x": bf(np.random.standard_normal((B, C, H, W)) * s[None, :, None, None]),
        "w_c1": bf(np.random.standard_normal((M, C)) / np.sqrt(C) * t[:, None] / s[None, :]),
        "b_c1": bf(np.random.standard_normal(M) * 0.3 * t),
        "w_q": bf(np.random.standard_normal((O, M)) / np.sqrt(M) / t[None, :]),
        "w_k": bf(np.random.standard_normal((O, M)) / np.sqrt(M) / t[None, :]),
        "w_v": bf(np.random.standard_normal((O, M)) / np.sqrt(M) / t[None, :]),
        "bn_gamma": bf(1.0 + 0.1 * np.random.standard_normal(O)),
        "bn_beta": bf(0.3 * np.random.standard_normal(O)),
        "prelu_a": bf(np.random.uniform(0.15, 0.35, (1,))),
    }


def reference(x, w_c1, b_c1, w_q, w_k, w_v, bn_gamma, bn_beta, prelu_a):
    ll = haar_ll(f64(x)).reshape(B, C, H2 * W2)
    y = (mxq(f64(w_c1), 1, "e4m3") @ mxq(ll, 1, "e4m3")) + f64(b_c1)[None, :, None]
    yq = mxq(y, 1, "e4m3")
    q = (mxq(f64(w_q), 1, "e4m3") @ yq).reshape(B, O, H2, W2)
    k = (mxq(f64(w_k), 1, "e4m3") @ yq).reshape(B, O, H2, W2)
    v = (mxq(f64(w_v), 1, "e4m3") @ yq).reshape(B, O, H2, W2)
    kw = windows(k)
    vw = windows(v)
    z = q[..., None] * kw
    e = np.exp(z - z.max(-1, keepdims=True))
    attn = e / e.sum(-1, keepdims=True)
    att = (attn * vw).sum(-1)
    m = att.mean(axis=(0, 2, 3), keepdims=True)
    var = att.var(axis=(0, 2, 3), keepdims=True)
    n = f64(bn_gamma)[None, :, None, None] * (att - m) / np.sqrt(var + BN_EPS) + f64(bn_beta)[None, :, None, None]
    return np.where(n >= 0, n, f64(prelu_a) * n)

@@ -1,0 +1,267 @@
+from contextlib import ExitStack
+
+import concourse.mybir as mybir
+from concourse.masks import make_identity
+
+F32 = mybir.dt.float32
+BF16 = mybir.dt.bfloat16
+I32 = mybir.dt.int32
+U8 = mybir.dt.uint8
+FP8X4 = mybir.dt.float8_e4m3fn_x4
+ALU = mybir.AluOpType
+ACT = mybir.ActivationFunctionType
+
+P = 128
+NB = 4
+NPIX = 1024
+ROW = 64
+STEPS = 8
+BN_EPS = 1e-5
+BANK_DT = F32
+
+FLOPS = 4 * 2 * 512 * 512 * 1024
+
+
+def tile_merge_pa_kernel(tc, x, w_c1, b_c1, w_q, w_k, w_v, bn_gamma, bn_beta, prelu_a, out):
+    nc = tc.nc
+    with ExitStack() as ctx:
+        keep = ctx.enter_context(tc.tile_pool(name="keep", bufs=1))
+
+        ident = keep.tile([P, P], F32, name="ident")
+        make_identity(nc, ident[:])
+
+        w_codes = []
+        w_scales = []
+        for i in range(4):
+            wct = keep.tile([P, 512], I32, name="w_codes%d" % i, align_bytes=64)
+            wst = keep.tile([P, 512], U8, name="w_scales%d" % i, align_bytes=64)
+            w_codes.append(wct)
+            w_scales.append(wst)
+        ll_codes = keep.tile([P, NPIX], I32, name="ll_codes", align_bytes=64)
+        ll_scales = keep.tile([P, NPIX], U8, name="ll_scales", align_bytes=64)
+        y_codes = []
+        y_scales = []
+        for d in range(3):
+            yct = keep.tile([P, NPIX + 2 * ROW], I32, name="y_codes%d" % d, align_bytes=64)
+            yst = keep.tile([P, NPIX + 2 * ROW], U8, name="y_scales%d" % d, align_bytes=64)
+            for c0 in (0, ROW + NPIX):
+                nc.vector.memset(yct[:, c0:c0 + ROW], 0)
+                nc.vector.memset(yst[:, c0:c0 + ROW].bitcast(I32), 0)
+            y_codes.append(yct)
+            y_scales.append(yst)
+
+        att = keep.tile([P, 4, NPIX], F32, name="att")
+        stats = keep.tile([P, 4, STEPS, 6], F32, name="stats")
+
+        bias_bf = keep.tile([P, 4], BF16, name="bias_bf")
+        gam_bf = keep.tile([P, 4], BF16, name="gam_bf")
+        bet_bf = keep.tile([P, 4], BF16, name="bet_bf")
+        a_bf = keep.tile([P, 1], BF16, name="a_bf")
+        nc.gpsimd.dma_start(out=bias_bf[:], in_=b_c1.rearrange("(p t) -> p t", t=4))
+        nc.gpsimd.dma_start(out=gam_bf[:], in_=bn_gamma.rearrange("(p t) -> p t", t=4))
+        nc.gpsimd.dma_start(out=bet_bf[:], in_=bn_beta.rearrange("(p t) -> p t", t=4))
+        nc.gpsimd.dma_start(out=a_bf[:], in_=prelu_a.partition_broadcast(P))
+        a_col = keep.tile([P, 1], F32, name="a_col")
+        nc.vector.tensor_copy(out=a_col[:], in_=a_bf[:])
+        zeros_bf = keep.tile([P, P], BF16, name="zeros_bf")
+        nc.vector.memset(zeros_bf[:], 0.0)
+        bias_full = keep.tile([P, P, 4], BF16, name="bias_full")
+        for t in range(4):
+            nc.vector.tensor_scalar(out=bias_full[:, :, t], in0=zeros_bf[:], scalar1=bias_bf[:, t:t + 1],
+                                    scalar2=None, op0=ALU.add)
+
+        with tc.tile_pool(name="head", bufs=1) as head, tc.psum_pool(name="psh", bufs=2) as psh:
+            weights = (w_c1, w_k, w_q, w_v)
+            x_sb = []
+            w_sb = []
+            for b in range(NB):
+                xt = head.tile([P, 4, 1024], BF16, name="x_sb%d" % b)
+                nc.sync.dma_start(out=xt[:], in_=x[b].rearrange("(p j) h w -> p j (h w)", j=4))
+                x_sb.append(xt)
+                wt = head.tile([P, 4, 512], BF16, name="w_sb%d" % b)
+                nc.sync.dma_start(out=wt[:], in_=weights[b].rearrange("(c r) k -> c r k", r=4))
+                w_sb.append(wt)
+
+            ll = head.tile([P, NPIX, 4], BF16, name="ll", align_bytes=64)
+            y_mid = head.tile([P, NPIX, 4], BF16, name="y_mid", align_bytes=64)
+            y_left = head.tile([P, NPIX, 4], BF16, name="y_left", align_bytes=64)
+            y_right = head.tile([P, NPIX, 4], BF16, name="y_right", align_bytes=64)
+            nc.gpsimd.memset(y_left[:], 0.0)
+            nc.gpsimd.memset(y_right[:], 0.0)
+            ll_by_image = ll[:].rearrange("p (y b x) j -> p b y x j", b=NB, x=16)
+
+            for b in range(NB):
+                rows = x_sb[b][:].rearrange("p j (i a w) -> p (j i) a w", a=2, w=32)
+                s1 = head.tile([P, 64, 32], F32, name="s1", tag="s1", bufs=2)
+                nc.vector.tensor_tensor(out=s1[:], in0=rows[:, :, 0, :], in1=rows[:, :, 1, :], op=ALU.add)
+                pairs = s1[:].rearrange("p r (x e) -> p (r x) e", e=2)
+                s2 = head.tile([P, 1024], F32, name="s2", tag="s2", bufs=2)
+                nc.vector.tensor_tensor(out=s2[:], in0=pairs[:, :, 0], in1=pairs[:, :, 1], op=ALU.add)
+                nc.scalar.activation(out=ll_by_image[:, b], in_=s2[:].rearrange("p (j y x) -> p y x j", j=4, x=16),
+                                     func=ACT.Copy, scale=0.5)
+
+                words = w_sb[b][:].bitcast(F32)
+                grouped = head.tile([P, 2048], BF16, name="grouped", tag="grouped", bufs=2, align_bytes=64)
+                gwords = grouped[:].bitcast(F32).rearrange("p (r c u) -> p r c u", r=4, u=2)
+                for h in range(2):
+                    wT = psh.tile([P, 2, 2, P], F32, name="wT", tag="wT")
+                    for rr in range(2):
+                        for u in range(2):
+                            nc.tensor.transpose(wT[:, rr, u, :], words[:, 2 * h + rr, u:256:2], ident[:])
+                    nc.scalar.copy(out=gwords[:, 2 * h:2 * h + 2], in_=wT[:].rearrange("p r u c -> p r c u"))
+                nc.vector.quantize_mx(out=w_codes[b][:].bitcast(FP8X4), scales=w_scales[b][:], in_=grouped[:])
+
+            ll_flat = ll[:].rearrange("p c j -> p (c j)")
+            lefts = y_left[:].rearrange("p (g x) t -> p g (x t)", x=16)
+            mids = y_mid[:].rearrange("p (g x) t -> p g (x t)", x=16)
+            rights = y_right[:].rearrange("p (g x) t -> p g (x t)", x=16)
+            for h in range(2):
+                nc.vector.quantize_mx(out=ll_codes[:, 512 * h:512 * (h + 1)].bitcast(FP8X4),
+                                      scales=ll_scales[:, 512 * h:512 * (h + 1)],
+                                      in_=ll_flat[:, 2048 * h:2048 * (h + 1)])
+                for r in range(4 * h, 4 * h + 4):
+                    cols = slice(P * r, P * (r + 1))
+                    bank = psh.tile([P, 4, P], BANK_DT, name="bank", tag="bank")
+                    for t in range(4):
+                        nc.tensor.matmul_mx(out=bank[:, t, :],
+                                            lhsT=w_codes[0][:, P * t:P * (t + 1)].bitcast(FP8X4),
+                                            lhsT_scale=w_scales[0][:, P * t:P * (t + 1)],
+                                            rhs=ll_codes[:, cols].bitcast(FP8X4), rhs_scale=ll_scales[:, cols],
+                                            start=True, stop=True)
+                    nc.vector.tensor_tensor(out=y_mid[:, cols, :], in0=bank[:].rearrange("p t n -> p n t"),
+                                            in1=bias_full[:], op=ALU.add)
+                g0 = 32 * h
+                nc.scalar.copy(out=lefts[:, g0:g0 + 32, 4:64], in_=mids[:, g0:g0 + 32, 0:60])
+                nc.scalar.copy(out=rights[:, g0:g0 + 32, 0:60], in_=mids[:, g0:g0 + 32, 4:64])
+                for d, ysrc in enumerate((y_left, y_mid, y_right)):
+                    c0 = ROW + 512 * h
+                    nc.vector.quantize_mx(out=y_codes[d][:, c0:c0 + 512].bitcast(FP8X4),
+                                          scales=y_scales[d][:, c0:c0 + 512],
+                                          in_=ysrc[:].rearrange("p c j -> p (c j)")[:, 2048 * h:2048 * (h + 1)])
+
+        with tc.tile_pool(name="main", bufs=2) as main, tc.psum_pool(name="psm", bufs=1) as psm:
+            zs = {}
+            evs = {}
+            nums = {}
+
+            def conv(dst, s, j, wi):
+                c0 = ROW + P * s + ROW * (j // 3 - 1)
+                d = j % 3
+                nc.tensor.matmul_mx(out=dst, lhsT=y_codes[d][:, c0:c0 + P].bitcast(FP8X4),
+                                    lhsT_scale=y_scales[d][:, c0:c0 + P],
+                                    rhs=w_codes[wi][:].bitcast(FP8X4), rhs_scale=w_scales[wi][:],
+                                    start=True, stop=True)
+
+            q_sbs = {}
+            rds = {}
+
+            def query(s):
+                q_ps = psm.tile([P, 512], F32, name="q_ps", tag="q_ps", bufs=1)
+                conv(q_ps[:], s, 4, 2)
+                q_sb = main.tile([P, 512], F32, name="q_sb", tag="q_sb")
+                nc.scalar.copy(out=q_sb[:], in_=q_ps[:])
+                q_sbs[s] = q_sb
+
+            def scores(s):
+                z = main.tile([P, 9, 512], F32, name="z", tag="z", bufs=3)
+                zs[s] = z
+                for j in range(9):
+                    k_ps = psm.tile([P, 512], F32, name="k_ps", tag="k_ps", bufs=3)
+                    conv(k_ps[:], s, j, 1)
+                    nc.vector.tensor_tensor(out=z[:, j, :], in0=q_sbs[s][:], in1=k_ps[:], op=ALU.mult)
+
+            def soft(s):
+                z = zs[s]
+                t1 = main.tile([P, 4, 512], F32, name="t1", tag="t1", bufs=1)
+                nc.vector.tensor_tensor(out=t1[:], in0=z[:, 0:4, :], in1=z[:, 4:8, :], op=ALU.max)
+                t2 = main.tile([P, 2, 512], F32, name="t2", tag="t2", bufs=1)
+                nc.vector.tensor_tensor(out=t2[:], in0=t1[:, 0:2, :], in1=t1[:, 2:4, :], op=ALU.max)
+                t3 = main.tile([P, 512], F32, name="t3", tag="t3", bufs=1)
+                nc.vector.tensor_tensor(out=t3[:], in0=t2[:, 0, :], in1=t2[:, 1, :], op=ALU.max)
+                m = main.tile([P, 512], F32, name="m", tag="m")
+                nc.vector.tensor_tensor(out=m[:], in0=t3[:], in1=z[:, 8, :], op=ALU.max)
+                for j in range(9):
+                    nc.gpsimd.tensor_tensor(out=z[:, j, :], in0=z[:, j, :], in1=m[:], op=ALU.subtract)
+                for g in range(3):
+                    nc.scalar.activation(out=z[:, 3 * g:3 * g + 3, :], in_=z[:, 3 * g:3 * g + 3, :], func=ACT.Exp)
+
+            def add_up(dst, src):
+                for ob in range(4):
+                    for j in range(9):
+                        nc.tensor.matmul(out=dst[:, ob, :], lhsT=src[:, j, P * ob:P * (ob + 1)], rhs=ident[:],
+                                         is_transpose=True, start=(j == 0), stop=(j == 8))
+
+            def weigh(s):
+                z = zs[s]
+                ev = main.tile([P, 9, 512], F32, name="ev", tag="ev", bufs=2)
+                evs[s] = ev
+                for j in range(9):
+                    v_ps = psm.tile([P, 512], F32, name="v_ps", tag="v_ps", bufs=2)
+                    conv(v_ps[:], s, j, 3)
+                    nc.vector.tensor_tensor(out=ev[:, j, :], in0=z[:, j, :], in1=v_ps[:], op=ALU.mult)
+
+            def numerator(s):
+                num = psm.tile([P, 4, P], F32, name="num", tag="num", bufs=1)
+                add_up(num, evs[s])
+                nums[s] = num
+
+            def denominator(s):
+                den = psm.tile([P, 4, P], F32, name="den", tag="den", bufs=1)
+                add_up(den, zs[s])
+                lg = main.tile([P, 4, P], F32, name="lg", tag="lg")
+                nc.scalar.activation(out=lg[:], in_=den[:], func=ACT.Ln)
+                rd = main.tile([P, 4, P], F32, name="rd", tag="rd")
+                nc.scalar.activation(out=rd[:], in_=lg[:], func=ACT.Exp, scale=-1.0)
+                rds[s] = rd
+
+            def divide(s):
+                cols = slice(P * s, P * (s + 1))
+                nc.vector.tensor_tensor(out=att[:, :, cols], in0=nums[s][:], in1=rds[s][:], op=ALU.mult)
+                for ob in range(4):
+                    nc.vector.bn_stats(out=stats[:, ob, s, :], in_=att[:, ob, cols])
+
+            query(0)
+            for s in range(STEPS + 2):
+                if s < STEPS:
+                    scores(s)
+                if s + 1 < STEPS:
+                    query(s + 1)
+                if s >= 2:
+                    weigh(s - 2)
+                if s < STEPS:
+                    soft(s)
+                if s >= 2:
+                    numerator(s - 2)
+                if 1 <= s <= STEPS:
+                    denominator(s - 1)
+                if s >= 2:
+                    divide(s - 2)
+
+            mv = main.tile([P, 4, 2], F32, name="mv", tag="mv", bufs=1)
+            for ob in range(4):
+                nc.vector.bn_aggr(out=mv[:, ob, :], in_=stats[:, ob, :, :].rearrange("p s k -> p (s k)"))
+            ve = main.tile([P, 4], F32, name="ve", tag="ve", bufs=1)
+            nc.vector.tensor_scalar(out=ve[:], in0=mv[:, :, 1], scalar1=BN_EPS, scalar2=None, op0=ALU.add)
+            sd = main.tile([P, 4], F32, name="sd", tag="sd", bufs=1)
+            nc.scalar.activation(out=sd[:], in_=ve[:], func=ACT.Sqrt)
+            rstd = main.tile([P, 4], F32, name="rstd", tag="rstd", bufs=1)
+            nc.vector.reciprocal(out=rstd[:], in_=sd[:])
+            gain = main.tile([P, 4], F32, name="gain", tag="gain", bufs=1)
+            nc.vector.tensor_tensor(out=gain[:], in0=gam_bf[:], in1=rstd[:], op=ALU.mult)
+            mg = main.tile([P, 4], F32, name="mg", tag="mg", bufs=1)
+            nc.vector.tensor_tensor(out=mg[:], in0=mv[:, :, 0], in1=gain[:], op=ALU.mult)
+            shift = main.tile([P, 4], F32, name="shift", tag="shift", bufs=1)
+            nc.vector.tensor_tensor(out=shift[:], in0=bet_bf[:], in1=mg[:], op=ALU.subtract)
+            out_v = out.rearrange("b (c r) h w -> c r b (h w)", r=4)
+            for ob in range(4):
+                n = main.tile([P, NPIX], F32, name="n", tag="n")
+                nc.scalar.activation(out=n[:].rearrange("p (b y x) -> p b y x", b=NB, x=16),
+                                     in_=att[:, ob, :].rearrange("p (y b x) -> p b y x", b=NB, x=16),
+                                     func=ACT.Identity, bias=shift[:, ob:ob + 1], scale=gain[:, ob:ob + 1])
+                neg = main.tile([P, NPIX], F32, name="neg", tag="neg")
+                nc.vector.tensor_scalar(out=neg[:], in0=n[:], scalar1=0.0, scalar2=a_col[:, 0:1],
+                                        op0=ALU.min, op1=ALU.mult)
+                res = main.tile([P, NPIX], F32, name="res", tag="res")
+                nc.vector.scalar_tensor_tensor(out=res[:], in0=n[:], scalar=0.0, in1=neg[:],
+                                               op0=ALU.max, op1=ALU.add)
+                nc.sync.dma_start(out=out_v[:, ob], in_=res[:].rearrange("p (b f) -> p b f", b=NB))

@@ -18,6 +18,8 @@ ROW = 64
 STEPS = 8
 BN_EPS = 1e-5
 BANK_DT = F32
+AHEAD = 3
+T_BURST = 6
 
 FLOPS = 4 * 2 * 512 * 512 * 1024
 
@@ -26,6 +28,7 @@ def tile_merge_pa_kernel(tc, x, w_c1, b_c1, w_q, w_k, w_v, bn_gamma, bn_beta, pr
     nc = tc.nc
     with ExitStack() as ctx:
         keep = ctx.enter_context(tc.tile_pool(name="keep", bufs=1))
+        mid = ctx.enter_context(tc.tile_pool(name="mid", bufs=1))
 
         ident = keep.tile([P, P], F32, name="ident")
         make_identity(nc, ident[:])
@@ -70,38 +73,87 @@ def tile_merge_pa_kernel(tc, x, w_c1, b_c1, w_q, w_k, w_v, bn_gamma, bn_beta, pr
             nc.vector.tensor_scalar(out=bias_full[:, :, t], in0=zeros_bf[:], scalar1=bias_bf[:, t:t + 1],
                                     scalar2=None, op0=ALU.add)
 
-        with tc.tile_pool(name="head", bufs=1) as head, tc.psum_pool(name="psh", bufs=2) as psh:
+        ll = mid.tile([P, NPIX, 4], BF16, name="ll", align_bytes=64)
+        y_mid = mid.tile([P, NPIX, 4], BF16, name="y_mid", align_bytes=64)
+        y_left = mid.tile([P, NPIX, 4], BF16, name="y_left", align_bytes=64)
+        y_right = mid.tile([P, NPIX, 4], BF16, name="y_right", align_bytes=64)
+        nc.gpsimd.memset(y_left[:], 0.0)
+        nc.gpsimd.memset(y_right[:], 0.0)
+        ll_by_image = ll[:].rearrange("p (y b x) j -> p b y x j", b=NB, x=16)
+        ll_flat = ll[:].rearrange("p c j -> p (c j)")
+        lefts = y_left[:].rearrange("p (g x) t -> p g (x t)", x=16)
+        mids = y_mid[:].rearrange("p (g x) t -> p g (x t)", x=16)
+        rights = y_right[:].rearrange("p (g x) t -> p g (x t)", x=16)
+
+        def quant_ll(h):
+            nc.vector.quantize_mx(out=ll_codes[:, 512 * h:512 * (h + 1)].bitcast(FP8X4),
+                                  scales=ll_scales[:, 512 * h:512 * (h + 1)],
+                                  in_=ll_flat[:, 2048 * h:2048 * (h + 1)])
+
+        def first_conv(bank, r):
+            cols = slice(P * r, P * (r + 1))
+            for t in range(4):
+                nc.tensor.matmul_mx(out=bank[:, t, :],
+                                    lhsT=w_codes[0][:, P * t:P * (t + 1)].bitcast(FP8X4),
+                                    lhsT_scale=w_scales[0][:, P * t:P * (t + 1)],
+                                    rhs=ll_codes[:, cols].bitcast(FP8X4), rhs_scale=ll_scales[:, cols],
+                                    start=True, stop=True)
+
+        def add_bias(bank, r):
+            nc.vector.tensor_tensor(out=y_mid[:, P * r:P * (r + 1), :], in0=bank[:].rearrange("p t n -> p n t"),
+                                    in1=bias_full[:], op=ALU.add)
+
+        def shift_copies(h):
+            g0 = 32 * h
+            nc.scalar.copy(out=lefts[:, g0:g0 + 32, 4:64], in_=mids[:, g0:g0 + 32, 0:60])
+            nc.scalar.copy(out=rights[:, g0:g0 + 32, 0:60], in_=mids[:, g0:g0 + 32, 4:64])
+
+        def quant_y(h):
+            c0 = ROW + 512 * h
+            for d, ysrc in enumerate((y_left, y_mid, y_right)):
+                nc.vector.quantize_mx(out=y_codes[d][:, c0:c0 + 512].bitcast(FP8X4),
+                                      scales=y_scales[d][:, c0:c0 + 512],
+                                      in_=ysrc[:].rearrange("p c j -> p (c j)")[:, 2048 * h:2048 * (h + 1)])
+
+        with tc.tile_pool(name="early", bufs=1) as early, tc.psum_pool(name="psh", bufs=2) as psh:
             weights = (w_c1, w_k, w_q, w_v)
             x_sb = []
             w_sb = []
-            for b in range(NB):
-                xt = head.tile([P, 4, 1024], BF16, name="x_sb%d" % b)
-                nc.sync.dma_start(out=xt[:], in_=x[b].rearrange("(p j) h w -> p j (h w)", j=4))
+            for i in range(4):
+                xt = early.tile([P, 4, 1024], BF16, name="x_sb%d" % i)
                 x_sb.append(xt)
-                wt = head.tile([P, 4, 512], BF16, name="w_sb%d" % b)
-                nc.sync.dma_start(out=wt[:], in_=weights[b].rearrange("(c r) k -> c r k", r=4))
+                wt = early.tile([P, 4, 512], BF16, name="w_sb%d" % i)
                 w_sb.append(wt)
 
-            ll = head.tile([P, NPIX, 4], BF16, name="ll", align_bytes=64)
-            y_mid = head.tile([P, NPIX, 4], BF16, name="y_mid", align_bytes=64)
-            y_left = head.tile([P, NPIX, 4], BF16, name="y_left", align_bytes=64)
-            y_right = head.tile([P, NPIX, 4], BF16, name="y_right", align_bytes=64)
-            nc.gpsimd.memset(y_left[:], 0.0)
-            nc.gpsimd.memset(y_right[:], 0.0)
-            ll_by_image = ll[:].rearrange("p (y b x) j -> p b y x j", b=NB, x=16)
+            def load_w(i):
+                nc.sync.dma_start(out=w_sb[i][:], in_=weights[i].rearrange("(c r) k -> c r k", r=4))
 
+            def load_x(b, h):
+                nc.sync.dma_start(out=x_sb[b][:, :, 512 * h:512 * (h + 1)],
+                                  in_=x[b].rearrange("(p j) h w -> p j (h w)", j=4)[:, :, 512 * h:512 * (h + 1)])
+
+            load_w(0)
             for b in range(NB):
-                rows = x_sb[b][:].rearrange("p j (i a w) -> p (j i) a w", a=2, w=32)
-                s1 = head.tile([P, 64, 32], F32, name="s1", tag="s1", bufs=2)
-                nc.vector.tensor_tensor(out=s1[:], in0=rows[:, :, 0, :], in1=rows[:, :, 1, :], op=ALU.add)
-                pairs = s1[:].rearrange("p r (x e) -> p (r x) e", e=2)
-                s2 = head.tile([P, 1024], F32, name="s2", tag="s2", bufs=2)
+                load_x(b, 0)
+            for i in range(1, 4):
+                load_w(i)
+            for b in range(NB):
+                load_x(b, 1)
+
+            def haar(b, h):
+                rows = x_sb[b][:, :, 512 * h:512 * (h + 1)].rearrange("p j (i a w) -> p j i a w", a=2, w=32)
+                s1 = early.tile([P, 4, 8, 32], F32, name="s1", tag="s1", bufs=2)
+                nc.vector.tensor_tensor(out=s1[:], in0=rows[:, :, :, 0, :], in1=rows[:, :, :, 1, :], op=ALU.add)
+                pairs = s1[:].rearrange("p j i (x e) -> p (j i x) e", e=2)
+                s2 = early.tile([P, 512], F32, name="s2", tag="s2", bufs=2)
                 nc.vector.tensor_tensor(out=s2[:], in0=pairs[:, :, 0], in1=pairs[:, :, 1], op=ALU.add)
-                nc.scalar.activation(out=ll_by_image[:, b], in_=s2[:].rearrange("p (j y x) -> p y x j", j=4, x=16),
+                nc.scalar.activation(out=ll_by_image[:, b, 8 * h:8 * (h + 1)],
+                                     in_=s2[:].rearrange("p (j y x) -> p y x j", j=4, x=16),
                                      func=ACT.Copy, scale=0.5)
 
-                words = w_sb[b][:].bitcast(F32)
-                grouped = head.tile([P, 2048], BF16, name="grouped", tag="grouped", bufs=2, align_bytes=64)
+            def prep_weight(i):
+                words = w_sb[i][:].bitcast(F32)
+                grouped = early.tile([P, 2048], BF16, name="grouped", tag="grouped", bufs=2, align_bytes=64)
                 gwords = grouped[:].bitcast(F32).rearrange("p (r c u) -> p r c u", r=4, u=2)
                 for h in range(2):
                     wT = psh.tile([P, 2, 2, P], F32, name="wT", tag="wT")
@@ -109,40 +161,34 @@ def tile_merge_pa_kernel(tc, x, w_c1, b_c1, w_q, w_k, w_v, bn_gamma, bn_beta, pr
                         for u in range(2):
                             nc.tensor.transpose(wT[:, rr, u, :], words[:, 2 * h + rr, u:256:2], ident[:])
                     nc.scalar.copy(out=gwords[:, 2 * h:2 * h + 2], in_=wT[:].rearrange("p r u c -> p r c u"))
-                nc.vector.quantize_mx(out=w_codes[b][:].bitcast(FP8X4), scales=w_scales[b][:], in_=grouped[:])
+                nc.vector.quantize_mx(out=w_codes[i][:].bitcast(FP8X4), scales=w_scales[i][:], in_=grouped[:])
 
-            ll_flat = ll[:].rearrange("p c j -> p (c j)")
-            lefts = y_left[:].rearrange("p (g x) t -> p g (x t)", x=16)
-            mids = y_mid[:].rearrange("p (g x) t -> p g (x t)", x=16)
-            rights = y_right[:].rearrange("p (g x) t -> p g (x t)", x=16)
-            for h in range(2):
-                nc.vector.quantize_mx(out=ll_codes[:, 512 * h:512 * (h + 1)].bitcast(FP8X4),
-                                      scales=ll_scales[:, 512 * h:512 * (h + 1)],
-                                      in_=ll_flat[:, 2048 * h:2048 * (h + 1)])
-                for r in range(4 * h, 4 * h + 4):
-                    cols = slice(P * r, P * (r + 1))
-                    bank = psh.tile([P, 4, P], BANK_DT, name="bank", tag="bank")
-                    for t in range(4):
-                        nc.tensor.matmul_mx(out=bank[:, t, :],
-                                            lhsT=w_codes[0][:, P * t:P * (t + 1)].bitcast(FP8X4),
-                                            lhsT_scale=w_scales[0][:, P * t:P * (t + 1)],
-                                            rhs=ll_codes[:, cols].bitcast(FP8X4), rhs_scale=ll_scales[:, cols],
-                                            start=True, stop=True)
-                    nc.vector.tensor_tensor(out=y_mid[:, cols, :], in0=bank[:].rearrange("p t n -> p n t"),
-                                            in1=bias_full[:], op=ALU.add)
-                g0 = 32 * h
-                nc.scalar.copy(out=lefts[:, g0:g0 + 32, 4:64], in_=mids[:, g0:g0 + 32, 0:60])
-                nc.scalar.copy(out=rights[:, g0:g0 + 32, 0:60], in_=mids[:, g0:g0 + 32, 4:64])
-                for d, ysrc in enumerate((y_left, y_mid, y_right)):
-                    c0 = ROW + 512 * h
-                    nc.vector.quantize_mx(out=y_codes[d][:, c0:c0 + 512].bitcast(FP8X4),
-                                          scales=y_scales[d][:, c0:c0 + 512],
-                                          in_=ysrc[:].rearrange("p c j -> p (c j)")[:, 2048 * h:2048 * (h + 1)])
+            prep_weight(0)
+            for b in range(NB):
+                haar(b, 0)
+            quant_ll(0)
+            for r in range(4):
+                bank = psh.tile([P, 4, P], BANK_DT, name="bank", tag="bank")
+                first_conv(bank, r)
+                add_bias(bank, r)
+            for i in range(1, 4):
+                prep_weight(i)
+            shift_copies(0)
+            quant_y(0)
+            for b in range(NB):
+                haar(b, 1)
 
         with tc.tile_pool(name="main", bufs=2) as main, tc.psum_pool(name="psm", bufs=1) as psm:
             zs = {}
             evs = {}
             nums = {}
+            dens = {}
+            q_sbs = {}
+            rds = {}
+            banks = {}
+
+            def ok(s):
+                return 0 <= s < STEPS
 
             def conv(dst, s, j, wi):
                 c0 = ROW + P * s + ROW * (j // 3 - 1)
@@ -152,25 +198,91 @@ def tile_merge_pa_kernel(tc, x, w_c1, b_c1, w_q, w_k, w_v, bn_gamma, bn_beta, pr
                                     rhs=w_codes[wi][:].bitcast(FP8X4), rhs_scale=w_scales[wi][:],
                                     start=True, stop=True)
 
-            q_sbs = {}
-            rds = {}
+            pe_list = [("q", 0, 0)] + [("k", 0, j) for j in range(AHEAD)]
+            for s in range(STEPS + 2):
+                mms = []
+                if ok(s):
+                    mms.extend([("k", s, j) for j in range(AHEAD, 9)])
+                if ok(s + 1):
+                    mms.append(("q", s + 1, 0))
+                if s == 1:
+                    mms.extend([("c", r, 0) for r in range(4, 8)])
+                sums = []
+                if ok(s - 2):
+                    mms.extend([("v", s - 2, j) for j in range(AHEAD, 9)])
+                    sums = [("F", s - 2, i) for i in range(36)]
+                for n, tok in enumerate(mms):
+                    pe_list.append(tok)
+                    if n % 2 == 1:
+                        pe_list.extend(sums[:T_BURST])
+                        sums = sums[T_BURST:]
+                pe_list.extend(sums)
+                if ok(s + 1):
+                    pe_list.extend([("k", s + 1, j) for j in range(AHEAD)])
+                if ok(s - 1):
+                    pe_list.extend([("v", s - 1, j) for j in range(AHEAD)])
+                if ok(s - 2):
+                    pe_list.extend([("G", s - 2, i) for i in range(36)])
 
-            def query(s):
-                q_ps = psm.tile([P, 512], F32, name="q_ps", tag="q_ps", bufs=1)
-                conv(q_ps[:], s, 4, 2)
+            def add_up(dst, src, i):
+                ob = i // 9
+                j = i % 9
+                nc.tensor.matmul(out=dst[:, ob, :], lhsT=src[:, j, P * ob:P * (ob + 1)], rhs=ident[:],
+                                 is_transpose=True, start=(j == 0), stop=(j == 8))
+
+            def emit_pe(tok):
+                kind, s, j = tok
+                if kind == "q":
+                    q_ps = psm.tile([P, 512], F32, name="q_ps", tag="k_ps", bufs=3)
+                    conv(q_ps[:], s, 4, 2)
+                    banks[tok] = q_ps
+                elif kind == "k":
+                    k_ps = psm.tile([P, 512], F32, name="k_ps", tag="k_ps", bufs=3)
+                    conv(k_ps[:], s, j, 1)
+                    banks[tok] = k_ps
+                elif kind == "v":
+                    v_ps = psm.tile([P, 512], F32, name="v_ps", tag="v_ps", bufs=3)
+                    conv(v_ps[:], s, j, 3)
+                    banks[tok] = v_ps
+                elif kind == "c":
+                    bank2 = psm.tile([P, 4, P], BANK_DT, name="bank2", tag="v_ps", bufs=3)
+                    first_conv(bank2, s)
+                    banks[tok] = bank2
+                elif kind == "F":
+                    if j == 0:
+                        den = psm.tile([P, 4, P], F32, name="den", tag="den", bufs=1)
+                        dens[s] = den
+                    add_up(dens[s], zs[s], j)
+                else:
+                    if j == 0:
+                        num = psm.tile([P, 4, P], F32, name="num", tag="num", bufs=1)
+                        nums[s] = num
+                    add_up(nums[s], evs[s], j)
+
+            done = set()
+            pos = [0]
+
+            def pump_to(tok):
+                while tok not in done:
+                    nxt = pe_list[pos[0]]
+                    pos[0] += 1
+                    emit_pe(nxt)
+                    done.add(nxt)
+
+            def q_copy(s):
+                pump_to(("q", s, 0))
                 q_sb = main.tile([P, 512], F32, name="q_sb", tag="q_sb")
-                nc.scalar.copy(out=q_sb[:], in_=q_ps[:])
+                nc.scalar.copy(out=q_sb[:], in_=banks[("q", s, 0)][:])
                 q_sbs[s] = q_sb
 
             def scores(s):
                 z = main.tile([P, 9, 512], F32, name="z", tag="z", bufs=3)
                 zs[s] = z
                 for j in range(9):
-                    k_ps = psm.tile([P, 512], F32, name="k_ps", tag="k_ps", bufs=3)
-                    conv(k_ps[:], s, j, 1)
-                    nc.vector.tensor_tensor(out=z[:, j, :], in0=q_sbs[s][:], in1=k_ps[:], op=ALU.mult)
+                    pump_to(("k", s, j))
+                    nc.vector.tensor_tensor(out=z[:, j, :], in0=q_sbs[s][:], in1=banks[("k", s, j)][:], op=ALU.mult)
 
-            def soft(s):
+            def shift_by_max(s):
                 z = zs[s]
                 t1 = main.tile([P, 4, 512], F32, name="t1", tag="t1", bufs=1)
                 nc.vector.tensor_tensor(out=t1[:], in0=z[:, 0:4, :], in1=z[:, 4:8, :], op=ALU.max)
@@ -182,60 +294,77 @@ def tile_merge_pa_kernel(tc, x, w_c1, b_c1, w_q, w_k, w_v, bn_gamma, bn_beta, pr
                 nc.vector.tensor_tensor(out=m[:], in0=t3[:], in1=z[:, 8, :], op=ALU.max)
                 for j in range(9):
                     nc.gpsimd.tensor_tensor(out=z[:, j, :], in0=z[:, j, :], in1=m[:], op=ALU.subtract)
-                for g in range(3):
-                    nc.scalar.activation(out=z[:, 3 * g:3 * g + 3, :], in_=z[:, 3 * g:3 * g + 3, :], func=ACT.Exp)
 
-            def add_up(dst, src):
-                for ob in range(4):
-                    for j in range(9):
-                        nc.tensor.matmul(out=dst[:, ob, :], lhsT=src[:, j, P * ob:P * (ob + 1)], rhs=ident[:],
-                                         is_transpose=True, start=(j == 0), stop=(j == 8))
-
-            def weigh(s):
+            def exps(s, g):
                 z = zs[s]
-                ev = main.tile([P, 9, 512], F32, name="ev", tag="ev", bufs=2)
-                evs[s] = ev
-                for j in range(9):
-                    v_ps = psm.tile([P, 512], F32, name="v_ps", tag="v_ps", bufs=2)
-                    conv(v_ps[:], s, j, 3)
-                    nc.vector.tensor_tensor(out=ev[:, j, :], in0=z[:, j, :], in1=v_ps[:], op=ALU.mult)
+                nc.scalar.activation(out=z[:, 3 * g:3 * g + 3, :], in_=z[:, 3 * g:3 * g + 3, :], func=ACT.Exp)
 
-            def numerator(s):
-                num = psm.tile([P, 4, P], F32, name="num", tag="num", bufs=1)
-                add_up(num, evs[s])
-                nums[s] = num
+            def weigh(s, j0, j1):
+                if j0 == 0:
+                    ev = main.tile([P, 9, 512], F32, name="ev", tag="ev", bufs=2)
+                    evs[s] = ev
+                for j in range(j0, j1):
+                    pump_to(("v", s, j))
+                    nc.vector.tensor_tensor(out=evs[s][:, j, :], in0=zs[s][:, j, :], in1=banks[("v", s, j)][:],
+                                            op=ALU.mult)
 
-            def denominator(s):
-                den = psm.tile([P, 4, P], F32, name="den", tag="den", bufs=1)
-                add_up(den, zs[s])
+            def one_over_den(s):
+                pump_to(("F", s, 35))
                 lg = main.tile([P, 4, P], F32, name="lg", tag="lg")
-                nc.scalar.activation(out=lg[:], in_=den[:], func=ACT.Ln)
+                nc.scalar.activation(out=lg[:], in_=dens[s][:], func=ACT.Ln)
                 rd = main.tile([P, 4, P], F32, name="rd", tag="rd")
                 nc.scalar.activation(out=rd[:], in_=lg[:], func=ACT.Exp, scale=-1.0)
                 rds[s] = rd
 
             def divide(s):
+                pump_to(("G", s, 35))
                 cols = slice(P * s, P * (s + 1))
                 nc.vector.tensor_tensor(out=att[:, :, cols], in0=nums[s][:], in1=rds[s][:], op=ALU.mult)
                 for ob in range(4):
                     nc.vector.bn_stats(out=stats[:, ob, s, :], in_=att[:, ob, cols])
 
-            query(0)
-            for s in range(STEPS + 2):
-                if s < STEPS:
+            warm = main.tile([P, 1], F32, name="warm", tag="warm", bufs=1)
+            with tc.manual_schedule():
+                q_copy(0)
+                for s in range(STEPS):
                     scores(s)
-                if s + 1 < STEPS:
-                    query(s + 1)
-                if s >= 2:
-                    weigh(s - 2)
-                if s < STEPS:
-                    soft(s)
-                if s >= 2:
-                    numerator(s - 2)
-                if 1 <= s <= STEPS:
-                    denominator(s - 1)
-                if s >= 2:
-                    divide(s - 2)
+                    if s == 1:
+                        for r in range(4, 8):
+                            pump_to(("c", r, 0))
+                            add_bias(banks[("c", r, 0)], r)
+                    if s == 2:
+                        quant_y(1)
+                    if ok(s - 3):
+                        divide(s - 3)
+                    if ok(s - 2):
+                        weigh(s - 2, 0, 9)
+                    shift_by_max(s)
+                    if s == 0:
+                        quant_ll(1)
+                    if ok(s - 1):
+                        exps(s - 1, 0)
+                    if ok(s + 1):
+                        q_copy(s + 1)
+                    if ok(s - 1):
+                        exps(s - 1, 1)
+                    if s == 1:
+                        shift_copies(1)
+                    if ok(s - 1):
+                        exps(s - 1, 2)
+                    if ok(s - 2):
+                        one_over_den(s - 2)
+                divide(STEPS - 3)
+                exps(STEPS - 1, 0)
+                weigh(STEPS - 2, 0, 9)
+                one_over_den(STEPS - 2)
+                exps(STEPS - 1, 1)
+                exps(STEPS - 1, 2)
+                weigh(STEPS - 1, 0, 6)
+                divide(STEPS - 2)
+                weigh(STEPS - 1, 6, 9)
+                one_over_den(STEPS - 1)
+                nc.scalar.activation(out=warm[:], in_=rds[STEPS - 1][:, 0, 0:1], func=ACT.Sqrt)
+                divide(STEPS - 1)
 
             mv = main.tile([P, 4, 2], F32, name="mv", tag="mv", bufs=1)
             for ob in range(4):

@@ -20,6 +20,7 @@ BN_EPS = 1e-5
 BANK_DT = F32
 AHEAD = 3
 T_BURST = 6
+ON_PE = ((3, 0), (2, 1), (3, 1))
 
 FLOPS = 4 * 2 * 512 * 512 * 1024
 
@@ -32,6 +33,8 @@ def tile_merge_pa_kernel(tc, x, w_c1, b_c1, w_q, w_k, w_v, bn_gamma, bn_beta, pr
 
         ident = keep.tile([P, P], F32, name="ident")
         make_identity(nc, ident[:])
+        ident_bf = keep.tile([P, P], BF16, name="ident_bf")
+        make_identity(nc, ident_bf[:])
 
         w_codes = []
         w_scales = []
@@ -54,7 +57,8 @@ def tile_merge_pa_kernel(tc, x, w_c1, b_c1, w_q, w_k, w_v, bn_gamma, bn_beta, pr
             y_scales.append(yst)
 
         att = keep.tile([P, 4, NPIX], F32, name="att")
-        stats = keep.tile([P, 4, STEPS, 6], F32, name="stats")
+        msums = keep.tile([P, 2, 4, STEPS], F32, name="msums")
+        neg_pivot = keep.tile([P, 4], F32, name="neg_pivot")
 
         bias_bf = keep.tile([P, 4], BF16, name="bias_bf")
         gam_bf = keep.tile([P, 4], BF16, name="gam_bf")
@@ -151,6 +155,16 @@ def tile_merge_pa_kernel(tc, x, w_c1, b_c1, w_q, w_k, w_v, bn_gamma, bn_beta, pr
                                      in_=s2[:].rearrange("p (j y x) -> p y x j", j=4, x=16),
                                      func=ACT.Copy, scale=0.5)
 
+            def haar_pe(b, h):
+                taps = x_sb[b][:, :, 512 * h:512 * (h + 1)].rearrange("p j (i a x e) -> p j i a x e", a=2, x=16, e=2)
+                hs = psh.tile([P, 512], F32, name="hs", tag="hs")
+                for n in range(4):
+                    nc.tensor.matmul(out=hs[:].rearrange("p (j i x) -> p j i x", j=4, x=16), lhsT=ident_bf[:],
+                                     rhs=taps[:, :, :, n // 2, :, n % 2], start=(n == 0), stop=(n == 3))
+                nc.scalar.activation(out=ll_by_image[:, b, 8 * h:8 * (h + 1)],
+                                     in_=hs[:].rearrange("p (j y x) -> p y x j", j=4, x=16),
+                                     func=ACT.Copy, scale=0.5)
+
             def prep_weight(i):
                 words = w_sb[i][:].bitcast(F32)
                 grouped = early.tile([P, 2048], BF16, name="grouped", tag="grouped", bufs=2, align_bytes=64)
@@ -165,7 +179,10 @@ def tile_merge_pa_kernel(tc, x, w_c1, b_c1, w_q, w_k, w_v, bn_gamma, bn_beta, pr
 
             prep_weight(0)
             for b in range(NB):
-                haar(b, 0)
+                if (b, 0) in ON_PE:
+                    haar_pe(b, 0)
+                else:
+                    haar(b, 0)
             quant_ll(0)
             for r in range(4):
                 bank = psh.tile([P, 4, P], BANK_DT, name="bank", tag="bank")
@@ -176,7 +193,10 @@ def tile_merge_pa_kernel(tc, x, w_c1, b_c1, w_q, w_k, w_v, bn_gamma, bn_beta, pr
             shift_copies(0)
             quant_y(0)
             for b in range(NB):
-                haar(b, 1)
+                if (b, 1) in ON_PE:
+                    haar_pe(b, 1)
+                else:
+                    haar(b, 1)
 
         with tc.tile_pool(name="main", bufs=2) as main, tc.psum_pool(name="psm", bufs=1) as psm:
             zs = {}
@@ -320,8 +340,18 @@ def tile_merge_pa_kernel(tc, x, w_c1, b_c1, w_q, w_k, w_v, bn_gamma, bn_beta, pr
                 pump_to(("G", s, 35))
                 cols = slice(P * s, P * (s + 1))
                 nc.vector.tensor_tensor(out=att[:, :, cols], in0=nums[s][:], in1=rds[s][:], op=ALU.mult)
+                if s == 0:
+                    nc.vector.tensor_scalar(out=neg_pivot[:], in0=att[:, :, 0], scalar1=-1.0, scalar2=None,
+                                            op0=ALU.mult)
+
+            def moments(s):
+                cols = slice(P * s, P * (s + 1))
                 for ob in range(4):
-                    nc.vector.bn_stats(out=stats[:, ob, s, :], in_=att[:, ob, cols])
+                    for kind, func in enumerate((ACT.Identity, ACT.Square)):
+                        junk = main.tile([P, P], F32, name="junk", tag="junk")
+                        nc.scalar.activation(out=junk[:], in_=att[:, ob, cols], func=func,
+                                             bias=neg_pivot[:, ob:ob + 1], scale=1.0,
+                                             accum_out=msums[:, kind, ob, s:s + 1])
 
             warm = main.tile([P, 1], F32, name="warm", tag="warm", bufs=1)
             with tc.manual_schedule():
@@ -345,6 +375,8 @@ def tile_merge_pa_kernel(tc, x, w_c1, b_c1, w_q, w_k, w_v, bn_gamma, bn_beta, pr
                         exps(s - 1, 0)
                     if ok(s + 1):
                         q_copy(s + 1)
+                    if ok(s - 3):
+                        moments(s - 3)
                     if ok(s - 1):
                         exps(s - 1, 1)
                     if s == 1:
@@ -355,22 +387,34 @@ def tile_merge_pa_kernel(tc, x, w_c1, b_c1, w_q, w_k, w_v, bn_gamma, bn_beta, pr
                         one_over_den(s - 2)
                 divide(STEPS - 3)
                 exps(STEPS - 1, 0)
+                moments(STEPS - 3)
                 weigh(STEPS - 2, 0, 9)
                 one_over_den(STEPS - 2)
                 exps(STEPS - 1, 1)
                 exps(STEPS - 1, 2)
                 weigh(STEPS - 1, 0, 6)
                 divide(STEPS - 2)
+                moments(STEPS - 2)
                 weigh(STEPS - 1, 6, 9)
                 one_over_den(STEPS - 1)
                 nc.scalar.activation(out=warm[:], in_=rds[STEPS - 1][:, 0, 0:1], func=ACT.Sqrt)
                 divide(STEPS - 1)
+                moments(STEPS - 1)
 
-            mv = main.tile([P, 4, 2], F32, name="mv", tag="mv", bufs=1)
-            for ob in range(4):
-                nc.vector.bn_aggr(out=mv[:, ob, :], in_=stats[:, ob, :, :].rearrange("p s k -> p (s k)"))
+            tot = main.tile([P, 2, 4], F32, name="tot", tag="tot", bufs=1)
+            nc.vector.tensor_reduce(out=tot[:].rearrange("p k o -> p (k o)"),
+                                    in_=msums[:].rearrange("p k o s -> p (k o) s"),
+                                    axis=mybir.AxisListType.X, op=ALU.add)
+            avg = main.tile([P, 2, 4], F32, name="avg", tag="avg", bufs=1)
+            nc.vector.tensor_scalar(out=avg[:], in0=tot[:], scalar1=1.0 / NPIX, scalar2=None, op0=ALU.mult)
+            dd = main.tile([P, 4], F32, name="dd", tag="dd", bufs=1)
+            nc.vector.tensor_tensor(out=dd[:], in0=avg[:, 0, :], in1=avg[:, 0, :], op=ALU.mult)
+            var = main.tile([P, 4], F32, name="var", tag="var", bufs=1)
+            nc.vector.tensor_tensor(out=var[:], in0=avg[:, 1, :], in1=dd[:], op=ALU.subtract)
             ve = main.tile([P, 4], F32, name="ve", tag="ve", bufs=1)
-            nc.vector.tensor_scalar(out=ve[:], in0=mv[:, :, 1], scalar1=BN_EPS, scalar2=None, op0=ALU.add)
+            nc.vector.tensor_scalar(out=ve[:], in0=var[:], scalar1=BN_EPS, scalar2=None, op0=ALU.add)
+            mean = main.tile([P, 4], F32, name="mean", tag="mean", bufs=1)
+            nc.vector.tensor_tensor(out=mean[:], in0=avg[:, 0, :], in1=neg_pivot[:], op=ALU.subtract)
             sd = main.tile([P, 4], F32, name="sd", tag="sd", bufs=1)
             nc.scalar.activation(out=sd[:], in_=ve[:], func=ACT.Sqrt)
             rstd = main.tile([P, 4], F32, name="rstd", tag="rstd", bufs=1)
@@ -378,7 +422,7 @@ def tile_merge_pa_kernel(tc, x, w_c1, b_c1, w_q, w_k, w_v, bn_gamma, bn_beta, pr
             gain = main.tile([P, 4], F32, name="gain", tag="gain", bufs=1)
             nc.vector.tensor_tensor(out=gain[:], in0=gam_bf[:], in1=rstd[:], op=ALU.mult)
             mg = main.tile([P, 4], F32, name="mg", tag="mg", bufs=1)
-            nc.vector.tensor_tensor(out=mg[:], in0=mv[:, :, 0], in1=gain[:], op=ALU.mult)
+            nc.vector.tensor_tensor(out=mg[:], in0=mean[:], in1=gain[:], op=ALU.mult)
             shift = main.tile([P, 4], F32, name="shift", tag="shift", bufs=1)
             nc.vector.tensor_tensor(out=shift[:], in0=bet_bf[:], in1=mg[:], op=ALU.subtract)
             out_v = out.rearrange("b (c r) h w -> c r b (h w)", r=4)

from contextlib import ExitStack

import concourse.mybir as mybir
from concourse.masks import make_identity

F32 = mybir.dt.float32
BF16 = mybir.dt.bfloat16
I32 = mybir.dt.int32
U8 = mybir.dt.uint8
FP8X4 = mybir.dt.float8_e4m3fn_x4
ALU = mybir.AluOpType
ACT = mybir.ActivationFunctionType

P = 128
NB = 4
NPIX = 1024
ROW = 64
STEPS = 8
BN_EPS = 1e-5
BANK_DT = F32
AHEAD = 3
T_BURST = 6
ON_PE = ((3, 0), (2, 1), (3, 1))

FLOPS = 4 * 2 * 512 * 512 * 1024


def tile_merge_pa_kernel(tc, x, w_c1, b_c1, w_q, w_k, w_v, bn_gamma, bn_beta, prelu_a, out):
    nc = tc.nc
    with ExitStack() as ctx:
        keep = ctx.enter_context(tc.tile_pool(name="keep", bufs=1))
        mid = ctx.enter_context(tc.tile_pool(name="mid", bufs=1))

        ident = keep.tile([P, P], F32, name="ident")
        make_identity(nc, ident[:])
        ident_bf = keep.tile([P, P], BF16, name="ident_bf")
        make_identity(nc, ident_bf[:])

        w_codes = []
        w_scales = []
        for i in range(4):
            wct = keep.tile([P, 512], I32, name="w_codes%d" % i, align_bytes=64)
            wst = keep.tile([P, 512], U8, name="w_scales%d" % i, align_bytes=64)
            w_codes.append(wct)
            w_scales.append(wst)
        ll_codes = keep.tile([P, NPIX], I32, name="ll_codes", align_bytes=64)
        ll_scales = keep.tile([P, NPIX], U8, name="ll_scales", align_bytes=64)
        y_codes = []
        y_scales = []
        for d in range(3):
            yct = keep.tile([P, NPIX + 2 * ROW], I32, name="y_codes%d" % d, align_bytes=64)
            yst = keep.tile([P, NPIX + 2 * ROW], U8, name="y_scales%d" % d, align_bytes=64)
            for c0 in (0, ROW + NPIX):
                nc.vector.memset(yct[:, c0:c0 + ROW], 0)
                nc.vector.memset(yst[:, c0:c0 + ROW].bitcast(I32), 0)
            y_codes.append(yct)
            y_scales.append(yst)

        att = keep.tile([P, 4, NPIX], F32, name="att")
        msums = keep.tile([P, 2, 4, STEPS], F32, name="msums")
        neg_pivot = keep.tile([P, 4], F32, name="neg_pivot")

        bias_bf = keep.tile([P, 4], BF16, name="bias_bf")
        gam_bf = keep.tile([P, 4], BF16, name="gam_bf")
        bet_bf = keep.tile([P, 4], BF16, name="bet_bf")
        a_bf = keep.tile([P, 1], BF16, name="a_bf")
        nc.gpsimd.dma_start(out=bias_bf[:], in_=b_c1.rearrange("(p t) -> p t", t=4))
        nc.gpsimd.dma_start(out=gam_bf[:], in_=bn_gamma.rearrange("(p t) -> p t", t=4))
        nc.gpsimd.dma_start(out=bet_bf[:], in_=bn_beta.rearrange("(p t) -> p t", t=4))
        nc.gpsimd.dma_start(out=a_bf[:], in_=prelu_a.partition_broadcast(P))
        a_col = keep.tile([P, 1], F32, name="a_col")
        nc.vector.tensor_copy(out=a_col[:], in_=a_bf[:])
        zeros_bf = keep.tile([P, P], BF16, name="zeros_bf")
        nc.vector.memset(zeros_bf[:], 0.0)
        bias_full = keep.tile([P, P, 4], BF16, name="bias_full")
        for t in range(4):
            nc.vector.tensor_scalar(out=bias_full[:, :, t], in0=zeros_bf[:], scalar1=bias_bf[:, t:t + 1],
                                    scalar2=None, op0=ALU.add)

        ll = mid.tile([P, NPIX, 4], BF16, name="ll", align_bytes=64)
        y_mid = mid.tile([P, NPIX, 4], BF16, name="y_mid", align_bytes=64)
        y_left = mid.tile([P, NPIX, 4], BF16, name="y_left", align_bytes=64)
        y_right = mid.tile([P, NPIX, 4], BF16, name="y_right", align_bytes=64)
        nc.gpsimd.memset(y_left[:], 0.0)
        nc.gpsimd.memset(y_right[:], 0.0)
        ll_by_image = ll[:].rearrange("p (y b x) j -> p b y x j", b=NB, x=16)
        ll_flat = ll[:].rearrange("p c j -> p (c j)")
        lefts = y_left[:].rearrange("p (g x) t -> p g (x t)", x=16)
        mids = y_mid[:].rearrange("p (g x) t -> p g (x t)", x=16)
        rights = y_right[:].rearrange("p (g x) t -> p g (x t)", x=16)

        def quant_ll(h):
            nc.vector.quantize_mx(out=ll_codes[:, 512 * h:512 * (h + 1)].bitcast(FP8X4),
                                  scales=ll_scales[:, 512 * h:512 * (h + 1)],
                                  in_=ll_flat[:, 2048 * h:2048 * (h + 1)])

        def first_conv(bank, r):
            cols = slice(P * r, P * (r + 1))
            for t in range(4):
                nc.tensor.matmul_mx(out=bank[:, t, :],
                                    lhsT=w_codes[0][:, P * t:P * (t + 1)].bitcast(FP8X4),
                                    lhsT_scale=w_scales[0][:, P * t:P * (t + 1)],
                                    rhs=ll_codes[:, cols].bitcast(FP8X4), rhs_scale=ll_scales[:, cols],
                                    start=True, stop=True)

        def add_bias(bank, r):
            nc.vector.tensor_tensor(out=y_mid[:, P * r:P * (r + 1), :], in0=bank[:].rearrange("p t n -> p n t"),
                                    in1=bias_full[:], op=ALU.add)

        def shift_copies(h):
            g0 = 32 * h
            nc.scalar.copy(out=lefts[:, g0:g0 + 32, 4:64], in_=mids[:, g0:g0 + 32, 0:60])
            nc.scalar.copy(out=rights[:, g0:g0 + 32, 0:60], in_=mids[:, g0:g0 + 32, 4:64])

        def quant_y(h):
            c0 = ROW + 512 * h
            for d, ysrc in enumerate((y_left, y_mid, y_right)):
                nc.vector.quantize_mx(out=y_codes[d][:, c0:c0 + 512].bitcast(FP8X4),
                                      scales=y_scales[d][:, c0:c0 + 512],
                                      in_=ysrc[:].rearrange("p c j -> p (c j)")[:, 2048 * h:2048 * (h + 1)])

        with tc.tile_pool(name="early", bufs=1) as early, tc.psum_pool(name="psh", bufs=2) as psh:
            weights = (w_c1, w_k, w_q, w_v)
            x_sb = []
            w_sb = []
            for i in range(4):
                xt = early.tile([P, 4, 1024], BF16, name="x_sb%d" % i)
                x_sb.append(xt)
                wt = early.tile([P, 4, 512], BF16, name="w_sb%d" % i)
                w_sb.append(wt)

            def load_w(i):
                nc.sync.dma_start(out=w_sb[i][:], in_=weights[i].rearrange("(c r) k -> c r k", r=4))

            def load_x(b, h):
                nc.sync.dma_start(out=x_sb[b][:, :, 512 * h:512 * (h + 1)],
                                  in_=x[b].rearrange("(p j) h w -> p j (h w)", j=4)[:, :, 512 * h:512 * (h + 1)])

            load_w(0)
            for b in range(NB):
                load_x(b, 0)
            for i in range(1, 4):
                load_w(i)
            for b in range(NB):
                load_x(b, 1)

            def haar(b, h):
                rows = x_sb[b][:, :, 512 * h:512 * (h + 1)].rearrange("p j (i a w) -> p j i a w", a=2, w=32)
                s1 = early.tile([P, 4, 8, 32], F32, name="s1", tag="s1", bufs=2)
                nc.vector.tensor_tensor(out=s1[:], in0=rows[:, :, :, 0, :], in1=rows[:, :, :, 1, :], op=ALU.add)
                pairs = s1[:].rearrange("p j i (x e) -> p (j i x) e", e=2)
                s2 = early.tile([P, 512], F32, name="s2", tag="s2", bufs=2)
                nc.vector.tensor_tensor(out=s2[:], in0=pairs[:, :, 0], in1=pairs[:, :, 1], op=ALU.add)
                nc.scalar.activation(out=ll_by_image[:, b, 8 * h:8 * (h + 1)],
                                     in_=s2[:].rearrange("p (j y x) -> p y x j", j=4, x=16),
                                     func=ACT.Copy, scale=0.5)

            def haar_pe(b, h):
                taps = x_sb[b][:, :, 512 * h:512 * (h + 1)].rearrange("p j (i a x e) -> p j i a x e", a=2, x=16, e=2)
                hs = psh.tile([P, 512], F32, name="hs", tag="hs")
                for n in range(4):
                    nc.tensor.matmul(out=hs[:].rearrange("p (j i x) -> p j i x", j=4, x=16), lhsT=ident_bf[:],
                                     rhs=taps[:, :, :, n // 2, :, n % 2], start=(n == 0), stop=(n == 3))
                nc.scalar.activation(out=ll_by_image[:, b, 8 * h:8 * (h + 1)],
                                     in_=hs[:].rearrange("p (j y x) -> p y x j", j=4, x=16),
                                     func=ACT.Copy, scale=0.5)

            def prep_weight(i):
                words = w_sb[i][:].bitcast(F32)
                grouped = early.tile([P, 2048], BF16, name="grouped", tag="grouped", bufs=2, align_bytes=64)
                gwords = grouped[:].bitcast(F32).rearrange("p (r c u) -> p r c u", r=4, u=2)
                for h in range(2):
                    wT = psh.tile([P, 2, 2, P], F32, name="wT", tag="wT")
                    for rr in range(2):
                        for u in range(2):
                            nc.tensor.transpose(wT[:, rr, u, :], words[:, 2 * h + rr, u:256:2], ident[:])
                    nc.scalar.copy(out=gwords[:, 2 * h:2 * h + 2], in_=wT[:].rearrange("p r u c -> p r c u"))
                nc.vector.quantize_mx(out=w_codes[i][:].bitcast(FP8X4), scales=w_scales[i][:], in_=grouped[:])

            prep_weight(0)
            for b in range(NB):
                if (b, 0) in ON_PE:
                    haar_pe(b, 0)
                else:
                    haar(b, 0)
            quant_ll(0)
            for r in range(4):
                bank = psh.tile([P, 4, P], BANK_DT, name="bank", tag="bank")
                first_conv(bank, r)
                add_bias(bank, r)
            for i in range(1, 4):
                prep_weight(i)
            shift_copies(0)
            quant_y(0)
            for b in range(NB):
                if (b, 1) in ON_PE:
                    haar_pe(b, 1)
                else:
                    haar(b, 1)

        with tc.tile_pool(name="main", bufs=2) as main, tc.psum_pool(name="psm", bufs=1) as psm:
            zs = {}
            evs = {}
            nums = {}
            dens = {}
            q_sbs = {}
            rds = {}
            banks = {}

            def ok(s):
                return 0 <= s < STEPS

            def conv(dst, s, j, wi):
                c0 = ROW + P * s + ROW * (j // 3 - 1)
                d = j % 3
                nc.tensor.matmul_mx(out=dst, lhsT=y_codes[d][:, c0:c0 + P].bitcast(FP8X4),
                                    lhsT_scale=y_scales[d][:, c0:c0 + P],
                                    rhs=w_codes[wi][:].bitcast(FP8X4), rhs_scale=w_scales[wi][:],
                                    start=True, stop=True)

            pe_list = [("q", 0, 0)] + [("k", 0, j) for j in range(AHEAD)]
            for s in range(STEPS + 2):
                mms = []
                if ok(s):
                    mms.extend([("k", s, j) for j in range(AHEAD, 9)])
                if ok(s + 1):
                    mms.append(("q", s + 1, 0))
                if s == 1:
                    mms.extend([("c", r, 0) for r in range(4, 8)])
                sums = []
                if ok(s - 2):
                    mms.extend([("v", s - 2, j) for j in range(AHEAD, 9)])
                    sums = [("F", s - 2, i) for i in range(36)]
                for n, tok in enumerate(mms):
                    pe_list.append(tok)
                    if n % 2 == 1:
                        pe_list.extend(sums[:T_BURST])
                        sums = sums[T_BURST:]
                pe_list.extend(sums)
                if ok(s + 1):
                    pe_list.extend([("k", s + 1, j) for j in range(AHEAD)])
                if ok(s - 1):
                    pe_list.extend([("v", s - 1, j) for j in range(AHEAD)])
                if ok(s - 2):
                    pe_list.extend([("G", s - 2, i) for i in range(36)])

            def add_up(dst, src, i):
                ob = i // 9
                j = i % 9
                nc.tensor.matmul(out=dst[:, ob, :], lhsT=src[:, j, P * ob:P * (ob + 1)], rhs=ident[:],
                                 is_transpose=True, start=(j == 0), stop=(j == 8))

            def emit_pe(tok):
                kind, s, j = tok
                if kind == "q":
                    q_ps = psm.tile([P, 512], F32, name="q_ps", tag="k_ps", bufs=3)
                    conv(q_ps[:], s, 4, 2)
                    banks[tok] = q_ps
                elif kind == "k":
                    k_ps = psm.tile([P, 512], F32, name="k_ps", tag="k_ps", bufs=3)
                    conv(k_ps[:], s, j, 1)
                    banks[tok] = k_ps
                elif kind == "v":
                    v_ps = psm.tile([P, 512], F32, name="v_ps", tag="v_ps", bufs=3)
                    conv(v_ps[:], s, j, 3)
                    banks[tok] = v_ps
                elif kind == "c":
                    bank2 = psm.tile([P, 4, P], BANK_DT, name="bank2", tag="v_ps", bufs=3)
                    first_conv(bank2, s)
                    banks[tok] = bank2
                elif kind == "F":
                    if j == 0:
                        den = psm.tile([P, 4, P], F32, name="den", tag="den", bufs=1)
                        dens[s] = den
                    add_up(dens[s], zs[s], j)
                else:
                    if j == 0:
                        num = psm.tile([P, 4, P], F32, name="num", tag="num", bufs=1)
                        nums[s] = num
                    add_up(nums[s], evs[s], j)

            done = set()
            pos = [0]

            def pump_to(tok):
                while tok not in done:
                    nxt = pe_list[pos[0]]
                    pos[0] += 1
                    emit_pe(nxt)
                    done.add(nxt)

            def q_copy(s):
                pump_to(("q", s, 0))
                q_sb = main.tile([P, 512], F32, name="q_sb", tag="q_sb")
                nc.scalar.copy(out=q_sb[:], in_=banks[("q", s, 0)][:])
                q_sbs[s] = q_sb

            def scores(s):
                z = main.tile([P, 9, 512], F32, name="z", tag="z", bufs=3)
                zs[s] = z
                for j in range(9):
                    pump_to(("k", s, j))
                    nc.vector.tensor_tensor(out=z[:, j, :], in0=q_sbs[s][:], in1=banks[("k", s, j)][:], op=ALU.mult)

            def shift_by_max(s):
                z = zs[s]
                t1 = main.tile([P, 4, 512], F32, name="t1", tag="t1", bufs=1)
                nc.vector.tensor_tensor(out=t1[:], in0=z[:, 0:4, :], in1=z[:, 4:8, :], op=ALU.max)
                t2 = main.tile([P, 2, 512], F32, name="t2", tag="t2", bufs=1)
                nc.vector.tensor_tensor(out=t2[:], in0=t1[:, 0:2, :], in1=t1[:, 2:4, :], op=ALU.max)
                t3 = main.tile([P, 512], F32, name="t3", tag="t3", bufs=1)
                nc.vector.tensor_tensor(out=t3[:], in0=t2[:, 0, :], in1=t2[:, 1, :], op=ALU.max)
                m = main.tile([P, 512], F32, name="m", tag="m")
                nc.vector.tensor_tensor(out=m[:], in0=t3[:], in1=z[:, 8, :], op=ALU.max)
                for j in range(9):
                    nc.gpsimd.tensor_tensor(out=z[:, j, :], in0=z[:, j, :], in1=m[:], op=ALU.subtract)

            def exps(s, g):
                z = zs[s]
                nc.scalar.activation(out=z[:, 3 * g:3 * g + 3, :], in_=z[:, 3 * g:3 * g + 3, :], func=ACT.Exp)

            def weigh(s, j0, j1):
                if j0 == 0:
                    ev = main.tile([P, 9, 512], F32, name="ev", tag="ev", bufs=2)
                    evs[s] = ev
                for j in range(j0, j1):
                    pump_to(("v", s, j))
                    nc.vector.tensor_tensor(out=evs[s][:, j, :], in0=zs[s][:, j, :], in1=banks[("v", s, j)][:],
                                            op=ALU.mult)

            def one_over_den(s):
                pump_to(("F", s, 35))
                lg = main.tile([P, 4, P], F32, name="lg", tag="lg")
                nc.scalar.activation(out=lg[:], in_=dens[s][:], func=ACT.Ln)
                rd = main.tile([P, 4, P], F32, name="rd", tag="rd")
                nc.scalar.activation(out=rd[:], in_=lg[:], func=ACT.Exp, scale=-1.0)
                rds[s] = rd

            def divide(s):
                pump_to(("G", s, 35))
                cols = slice(P * s, P * (s + 1))
                nc.vector.tensor_tensor(out=att[:, :, cols], in0=nums[s][:], in1=rds[s][:], op=ALU.mult)
                if s == 0:
                    nc.vector.tensor_scalar(out=neg_pivot[:], in0=att[:, :, 0], scalar1=-1.0, scalar2=None,
                                            op0=ALU.mult)

            def moments(s):
                cols = slice(P * s, P * (s + 1))
                for ob in range(4):
                    for kind, func in enumerate((ACT.Identity, ACT.Square)):
                        junk = main.tile([P, P], F32, name="junk", tag="junk")
                        nc.scalar.activation(out=junk[:], in_=att[:, ob, cols], func=func,
                                             bias=neg_pivot[:, ob:ob + 1], scale=1.0,
                                             accum_out=msums[:, kind, ob, s:s + 1])

            warm = main.tile([P, 1], F32, name="warm", tag="warm", bufs=1)
            with tc.manual_schedule():
                q_copy(0)
                for s in range(STEPS):
                    scores(s)
                    if s == 1:
                        for r in range(4, 8):
                            pump_to(("c", r, 0))
                            add_bias(banks[("c", r, 0)], r)
                    if s == 2:
                        quant_y(1)
                    if ok(s - 3):
                        divide(s - 3)
                    if ok(s - 2):
                        weigh(s - 2, 0, 9)
                    shift_by_max(s)
                    if s == 0:
                        quant_ll(1)
                    if ok(s - 1):
                        exps(s - 1, 0)
                    if ok(s + 1):
                        q_copy(s + 1)
                    if ok(s - 3):
                        moments(s - 3)
                    if ok(s - 1):
                        exps(s - 1, 1)
                    if s == 1:
                        shift_copies(1)
                    if ok(s - 1):
                        exps(s - 1, 2)
                    if ok(s - 2):
                        one_over_den(s - 2)
                divide(STEPS - 3)
                exps(STEPS - 1, 0)
                moments(STEPS - 3)
                weigh(STEPS - 2, 0, 9)
                one_over_den(STEPS - 2)
                exps(STEPS - 1, 1)
                exps(STEPS - 1, 2)
                weigh(STEPS - 1, 0, 6)
                divide(STEPS - 2)
                moments(STEPS - 2)
                weigh(STEPS - 1, 6, 9)
                one_over_den(STEPS - 1)
                nc.scalar.activation(out=warm[:], in_=rds[STEPS - 1][:, 0, 0:1], func=ACT.Sqrt)
                divide(STEPS - 1)
                moments(STEPS - 1)

            tot = main.tile([P, 2, 4], F32, name="tot", tag="tot", bufs=1)
            nc.vector.tensor_reduce(out=tot[:].rearrange("p k o -> p (k o)"),
                                    in_=msums[:].rearrange("p k o s -> p (k o) s"),
                                    axis=mybir.AxisListType.X, op=ALU.add)
            avg = main.tile([P, 2, 4], F32, name="avg", tag="avg", bufs=1)
            nc.vector.tensor_scalar(out=avg[:], in0=tot[:], scalar1=1.0 / NPIX, scalar2=None, op0=ALU.mult)
            dd = main.tile([P, 4], F32, name="dd", tag="dd", bufs=1)
            nc.vector.tensor_tensor(out=dd[:], in0=avg[:, 0, :], in1=avg[:, 0, :], op=ALU.mult)
            var = main.tile([P, 4], F32, name="var", tag="var", bufs=1)
            nc.vector.tensor_tensor(out=var[:], in0=avg[:, 1, :], in1=dd[:], op=ALU.subtract)
            ve = main.tile([P, 4], F32, name="ve", tag="ve", bufs=1)
            nc.vector.tensor_scalar(out=ve[:], in0=var[:], scalar1=BN_EPS, scalar2=None, op0=ALU.add)
            mean = main.tile([P, 4], F32, name="mean", tag="mean", bufs=1)
            nc.vector.tensor_tensor(out=mean[:], in0=avg[:, 0, :], in1=neg_pivot[:], op=ALU.subtract)
            sd = main.tile([P, 4], F32, name="sd", tag="sd", bufs=1)
            nc.scalar.activation(out=sd[:], in_=ve[:], func=ACT.Sqrt)
            rstd = main.tile([P, 4], F32, name="rstd", tag="rstd", bufs=1)
            nc.vector.reciprocal(out=rstd[:], in_=sd[:])
            gain = main.tile([P, 4], F32, name="gain", tag="gain", bufs=1)
            nc.vector.tensor_tensor(out=gain[:], in0=gam_bf[:], in1=rstd[:], op=ALU.mult)
            mg = main.tile([P, 4], F32, name="mg", tag="mg", bufs=1)
            nc.vector.tensor_tensor(out=mg[:], in0=mean[:], in1=gain[:], op=ALU.mult)
            shift = main.tile([P, 4], F32, name="shift", tag="shift", bufs=1)
            nc.vector.tensor_tensor(out=shift[:], in0=bet_bf[:], in1=mg[:], op=ALU.subtract)
            out_v = out.rearrange("b (c r) h w -> c r b (h w)", r=4)
            for ob in range(4):
                n = main.tile([P, NPIX], F32, name="n", tag="n")
                nc.scalar.activation(out=n[:].rearrange("p (b y x) -> p b y x", b=NB, x=16),
                                     in_=att[:, ob, :].rearrange("p (y b x) -> p b y x", b=NB, x=16),
                                     func=ACT.Identity, bias=shift[:, ob:ob + 1], scale=gain[:, ob:ob + 1])
                neg = main.tile([P, NPIX], F32, name="neg", tag="neg")
                nc.vector.tensor_scalar(out=neg[:], in0=n[:], scalar1=0.0, scalar2=a_col[:, 0:1],
                                        op0=ALU.min, op1=ALU.mult)
                res = main.tile([P, NPIX], F32, name="res", tag="res")
                nc.vector.scalar_tensor_tensor(out=res[:], in0=n[:], scalar=0.0, in1=neg[:],
                                               op0=ALU.max, op1=ALU.add)
                nc.sync.dma_start(out=out_v[:, ob], in_=res[:].rearrange("p (b f) -> p b f", b=NB))
